import numpy as np
import ml_dtypes


def mxq(x, axis, fmt="e4m3"):
    dtype, down = {"e4m3": (ml_dtypes.float8_e4m3fn, 7), "e5m2": (ml_dtypes.float8_e5m2, 14)}[fmt]
    v = np.moveaxis(np.asarray(x, np.float32).astype(ml_dtypes.bfloat16).astype(np.float64), axis, -1)
    blocks = v.reshape(v.shape[:-1] + (-1, 32))
    amax = np.abs(blocks).max(-1, keepdims=True)
    byte = np.maximum(np.where(amax > 0, np.frexp(amax)[1] - 1 + 127, 0) - down, 1)
    scale = np.exp2(byte - 127.0)
    codes = (blocks / scale).astype(np.float32).astype(dtype).astype(np.float64)
    return np.moveaxis((codes * scale).reshape(v.shape), -1, axis)


WIDE = False


def mx_kscale(k):
    if not WIDE:
        return np.ones(k)
    levels = np.array([10, -10, 5, -5, 0])
    a = np.random.permutation(np.resize(levels, k // 512 * 4)).reshape(k // 512, 4)
    idx = np.arange(k)
    return np.exp2(a[idx // 512, idx % 128 // 32])


BF16 = ml_dtypes.bfloat16


def bf(x):
    return np.asarray(x, np.float32).astype(BF16)


def f64(x):
    return np.asarray(x).astype(np.float64)


B, I, O = 128, 512, 256
DEGREE = 3
KNOTS = (0.2, 0.4, 0.6, 0.8)
SDIM = DEGREE + 1 + len(KNOTS)
T_MAX = 2.0


def truncated_power_basis(t):
    cols = [np.ones_like(t)]
    for p in range(1, DEGREE + 1):
        cols.append(t ** p)
    for c in KNOTS:
        cols.append(np.maximum(t - c, 0.0) ** DEGREE)
    return np.stack(cols, axis=1)


def setup_inputs():
    s = mx_kscale(I)
    t = np.random.random((B, 1)) * T_MAX
    x = np.random.random((B, I)) * s
    w = np.random.standard_normal((SDIM, I, O)) * (0.52 / np.sqrt(I)) / s[None, :, None]
    return {"inputs": bf(np.concatenate([t, x], axis=1)), "W_wts": bf(w.reshape(SDIM, I * O)),
            "b_wts": bf(np.random.standard_normal((SDIM, O)) * 0.3)}


def reference(inputs, W_wts, b_wts):
    inputs = f64(inputs)
    treatment = inputs[:, 0]
    features = inputs[:, 1:]
    basis = truncated_power_basis(treatment)
    Wk = f64(W_wts).reshape(SDIM, I, O)
    P = mxq(features, 1, "e4m3") @ mxq(Wk, 1, "e4m3")
    out = (basis.T[:, :, None] * P).sum(0)
    out = out + (basis[:, :, None] * f64(b_wts)[None, :, :]).sum(1)
    return out

@@ -1,0 +1,185 @@
+from contextlib import ExitStack
+
+import concourse.mybir as mybir
+from concourse.masks import make_identity
+
+F32 = mybir.dt.float32
+BF16 = mybir.dt.bfloat16
+U32 = mybir.dt.uint32
+U8 = mybir.dt.uint8
+FP8X4 = mybir.dt.float8_e4m3fn_x4
+ALU = mybir.AluOpType
+
+P = 128
+PACK = 4
+B, I, O = 128, 512, 256
+DEGREE = 3
+KNOTS = (0.2, 0.4, 0.6, 0.8)
+SDIM = DEGREE + 1 + len(KNOTS)
+RUN = 4
+
+VECTOR_OUTPUTS = (128, 72, 72, 72, 72, 72, 72, 72)
+
+BIAS_PARTS = 4
+BIAS_STEP = 6
+
+FLOPS = 2 * SDIM * B * I * O + 2 * B * SDIM * O
+
+assert I == P * PACK and B == P
+assert all(abs(knot - (k + 1) * KNOTS[0]) < 1e-12 for k, knot in enumerate(KNOTS))
+
+
+def regrouped(grouped, raw, outputs):
+    dst = grouped[:, outputs, :].rearrange("p (c r) t -> p c t r", r=RUN)
+    src = raw[:, :, outputs].rearrange("p t (c r) -> p c t r", r=RUN)
+    return dst, src
+
+
+def tile_vclinear_s_kernel(tc, inputs, W_wts, b_wts, out):
+    nc = tc.nc
+    with ExitStack() as ctx:
+        ctx.enter_context(tc.manual_schedule())
+        keep = ctx.enter_context(tc.tile_pool(name="keep", bufs=1))
+        setup_psum = ctx.enter_context(tc.psum_pool(name="setup_psum", bufs=1))
+        prod_psum = ctx.enter_context(tc.psum_pool(name="prod_psum", bufs=4))
+
+        warm = keep.tile([P, 2], F32)
+        nc.gpsimd.memset(warm[:, 0:1], 0.0)
+        nc.scalar.copy(out=warm[:, 1:2], in_=warm[:, 0:1])
+
+        t_sb = keep.tile([P, 32], BF16)
+        nc.sync.dma_start(out=t_sb[:], in_=inputs[:, 0:32])
+        t_col = t_sb[:, 0:1]
+        b_bf = keep.tile([SDIM, O], BF16)
+        nc.sync.dma_start(out=b_bf[:], in_=b_wts)
+        x_sb = keep.tile([P, I], BF16)
+        nc.sync.dma_start(out=x_sb[:], in_=inputs[:, 1 : 1 + I])
+        w_dram = W_wts.rearrange("s (p t o) -> p s t o", p=P, t=PACK)
+        w_raw = keep.tile([P, SDIM, PACK, O], BF16)
+        for s in range(SDIM):
+            nc.sync.dma_start(out=w_raw[:, s, :, :], in_=w_dram[:, s, :, :])
+
+        ident = keep.tile([P, P], F32)
+        make_identity(nc, ident[:])
+        basis = keep.tile([P, P], F32)
+        nc.vector.memset(basis[:], 0.0)
+        nc.vector.memset(basis[:, 0:1], 1.0)
+        b_f32 = keep.tile([P, O], F32)
+        nc.vector.memset(b_f32[:], 0.0)
+        knot_numbers = keep.tile([P, len(KNOTS)], F32)
+        for k in range(len(KNOTS)):
+            nc.vector.memset(knot_numbers[:, k : k + 1], float(k + 1))
+        nc.scalar.copy(out=b_f32[0:SDIM, :], in_=b_bf[:])
+
+        w_grouped = keep.tile([P, SDIM, O, PACK], BF16, align_bytes=64)
+        w_codes = keep.tile([P, SDIM, O], U32, align_bytes=64)
+        w_scales = keep.tile([P, SDIM, O], U8, align_bytes=64)
+        x_codes = keep.tile([P, B], U32, align_bytes=64)
+        x_scales = keep.tile([P, B], U8, align_bytes=64)
+        acc = keep.tile([B, O], F32)
+        prod_tiles = {}
+
+        def regroup(s):
+            split = VECTOR_OUTPUTS[s]
+            dst, src = regrouped(w_grouped[:, s, :, :], w_raw[:, s, :, :], slice(0, split))
+            nc.vector.tensor_copy(out=dst, in_=src)
+            cuts = (split, O // 2, O) if s == SDIM - 1 else (split, O)
+            for low, high in zip(cuts[:-1], cuts[1:]):
+                dst, src = regrouped(w_grouped[:, s, :, :], w_raw[:, s, :, :], slice(low, high))
+                nc.scalar.copy(out=dst, in_=src)
+
+        def multiply(s, outputs=slice(0, O)):
+            nc.vector.quantize_mx(
+                out=w_codes[:, s, outputs].bitcast(FP8X4),
+                scales=w_scales[:, s, outputs],
+                in_=w_grouped[:, s, outputs, :].rearrange("p o t -> p (o t)"),
+            )
+            prod = prod_psum.tile([B, O], F32, name="prod")
+            nc.tensor.matmul_mx(
+                out=prod[:, outputs],
+                lhsT=x_codes[:].bitcast(FP8X4),
+                lhsT_scale=x_scales[:],
+                rhs=w_codes[:, s, outputs].bitcast(FP8X4),
+                rhs_scale=w_scales[:, s, outputs],
+                start=True,
+                stop=True,
+            )
+            for start in range(outputs.start, outputs.stop, O // 2):
+                prod_tiles[(s, start)] = prod
+            if outputs.stop - outputs.start == O and s < BIAS_PARTS:
+                part = slice(s * (O // BIAS_PARTS), (s + 1) * (O // BIAS_PARTS))
+                nc.tensor.matmul(
+                    bias_psum[:, part], lhsT=basis_t[:], rhs=b_f32[:, part], start=True, stop=True
+                )
+
+        def accumulate(s, outputs=slice(0, O)):
+            if s == 0:
+                nc.vector.tensor_scalar_mul(out=acc[:], in0=prod_tiles[(s, 0)][:], scalar1=basis[:, 0:1])
+            else:
+                nc.vector.scalar_tensor_tensor(
+                    out=acc[:, outputs], in0=prod_tiles[(s, outputs.start)][:, outputs],
+                    scalar=basis[:, s : s + 1],
+                    in1=acc[:, outputs], op0=ALU.mult, op1=ALU.add,
+                )
+
+        distances = keep.tile([P, len(KNOTS)], F32)
+        squares = keep.tile([P, len(KNOTS)], F32)
+        nc.vector.scalar_tensor_tensor(
+            out=distances[:], in0=knot_numbers[:], scalar=-KNOTS[0],
+            in1=t_col.to_broadcast([P, len(KNOTS)]), op0=ALU.mult, op1=ALU.add,
+        )
+        nc.vector.tensor_copy(out=basis[:, 1:2], in_=t_col)
+        nc.vector.scalar_tensor_tensor(
+            out=squares[:], in0=distances[:], scalar=0.0, in1=distances[:], op0=ALU.max, op1=ALU.mult
+        )
+        nc.vector.tensor_scalar_mul(out=basis[:, 2:3], in0=t_col, scalar1=t_col)
+        nc.vector.scalar_tensor_tensor(
+            out=basis[:, DEGREE + 1 : SDIM], in0=distances[:], scalar=0.0, in1=squares[:],
+            op0=ALU.max, op1=ALU.mult,
+        )
+        nc.vector.tensor_scalar(
+            out=basis[:, 3:4], in0=t_col, scalar1=t_col, scalar2=t_col, op0=ALU.mult, op1=ALU.mult
+        )
+
+        x_words = x_sb[:].bitcast(F32).rearrange("p (w u) -> p u w", u=2)
+        x_t = setup_psum.tile([P, 2, B], F32)
+        for u in range(2):
+            nc.tensor.transpose(x_t[:, u, :], x_words[:, u, :], ident[:])
+        basis_t_psum = setup_psum.tile([P, B], F32)
+        nc.tensor.transpose(basis_t_psum[:], basis[:], ident[:])
+        x_grouped = keep.tile([P, B, PACK], BF16, align_bytes=64)
+        regroup(0)
+        nc.vector.tensor_copy(
+            out=x_grouped[:].rearrange("p b t -> p (b t)").bitcast(F32).rearrange("p (b u) -> p b u", u=2),
+            in_=x_t[:].rearrange("p u b -> p b u"),
+        )
+
+        basis_t = keep.tile([P, B], F32)
+        nc.vector.tensor_copy(out=basis_t[:], in_=basis_t_psum[:])
+        bias_psum = setup_psum.tile([B, O], F32)
+
+        regroup(1)
+        nc.vector.quantize_mx(
+            out=x_codes[:].bitcast(FP8X4),
+            scales=x_scales[:],
+            in_=x_grouped[:].rearrange("p b t -> p (b t)"),
+        )
+        multiply(0)
+
+        first, second = slice(0, O // 2), slice(O // 2, O)
+        for step in range(2, SDIM + 2):
+            if step < SDIM:
+                regroup(step)
+            if step >= 3:
+                accumulate(step - 3)
+            if step < SDIM:
+                multiply(step - 1)
+            if step == SDIM:
+                multiply(SDIM - 1, first)
+                multiply(SDIM - 1, second)
+            if step == BIAS_STEP:
+                nc.vector.tensor_add(out=acc[:], in0=acc[:], in1=bias_psum[:])
+        accumulate(SDIM - 1, first)
+        accumulate(SDIM - 1, second)
+
+        nc.sync.dma_start(out=out, in_=acc[:])

@@ -18,7 +18,7 @@ KNOTS = (0.2, 0.4, 0.6, 0.8)
 SDIM = DEGREE + 1 + len(KNOTS)
 RUN = 4
 
-VECTOR_OUTPUTS = (128, 72, 72, 72, 72, 72, 72, 72)
+VECTOR_OUTPUTS = (128, 56, 192, 56, 56, 56, 56, 16)
 
 BIAS_PARTS = 4
 BIAS_STEP = 6

@@ -18,7 +18,7 @@ KNOTS = (0.2, 0.4, 0.6, 0.8)
 SDIM = DEGREE + 1 + len(KNOTS)
 RUN = 4
 
-VECTOR_OUTPUTS = (128, 56, 192, 56, 56, 56, 56, 16)
+VECTOR_OUTPUTS = (128, 96, 96, 80, 80, 72, 64, 24)
 
 BIAS_PARTS = 4
 BIAS_STEP = 6
@@ -167,19 +167,24 @@ def tile_vclinear_s_kernel(tc, inputs, W_wts, b_wts, out):
         multiply(0)
 
         first, second = slice(0, O // 2), slice(O // 2, O)
-        for step in range(2, SDIM + 2):
-            if step < SDIM:
-                regroup(step)
+        halves = (first, second)
+        for step in range(2, SDIM - 1):
+            regroup(step)
             if step >= 3:
                 accumulate(step - 3)
-            if step < SDIM:
-                multiply(step - 1)
-            if step == SDIM:
-                multiply(SDIM - 1, first)
-                multiply(SDIM - 1, second)
-            if step == BIAS_STEP:
-                nc.vector.tensor_add(out=acc[:], in0=acc[:], in1=bias_psum[:])
-        accumulate(SDIM - 1, first)
-        accumulate(SDIM - 1, second)
+            multiply(step - 1)
+        regroup(SDIM - 1)
+        for half in halves:
+            nc.vector.tensor_add(out=acc[:, half], in0=acc[:, half], in1=bias_psum[:, half])
+        multiply(SDIM - 2)
+        for half in halves:
+            accumulate(4, half)
+        multiply(SDIM - 1, first)
+        for half in halves:
+            accumulate(5, half)
+        multiply(SDIM - 1, second)
+        for s in (6, 7):
+            for half in halves:
+                accumulate(s, half)
 
         nc.sync.dma_start(out=out, in_=acc[:])

@@ -21,7 +21,6 @@ RUN = 4
 VECTOR_OUTPUTS = (128, 96, 96, 80, 80, 72, 64, 24)
 
 BIAS_PARTS = 4
-BIAS_STEP = 6
 
 FLOPS = 2 * SDIM * B * I * O + 2 * B * SDIM * O
 
@@ -106,11 +105,8 @@ def tile_vclinear_s_kernel(tc, inputs, W_wts, b_wts, out):
             )
             for start in range(outputs.start, outputs.stop, O // 2):
                 prod_tiles[(s, start)] = prod
-            if outputs.stop - outputs.start == O and s < BIAS_PARTS:
-                part = slice(s * (O // BIAS_PARTS), (s + 1) * (O // BIAS_PARTS))
-                nc.tensor.matmul(
-                    bias_psum[:, part], lhsT=basis_t[:], rhs=b_f32[:, part], start=True, stop=True
-                )
+            if 1 <= s < BIAS_PARTS:
+                bias_matmul(s)
 
         def accumulate(s, outputs=slice(0, O)):
             if s == 0:
@@ -157,6 +153,14 @@ def tile_vclinear_s_kernel(tc, inputs, W_wts, b_wts, out):
         basis_t = keep.tile([P, B], F32)
         nc.vector.tensor_copy(out=basis_t[:], in_=basis_t_psum[:])
         bias_psum = setup_psum.tile([B, O], F32)
+
+        def bias_matmul(i):
+            part = slice(i * (O // BIAS_PARTS), (i + 1) * (O // BIAS_PARTS))
+            nc.tensor.matmul(
+                bias_psum[:, part], lhsT=basis_t[:], rhs=b_f32[:, part], start=True, stop=True
+            )
+
+        bias_matmul(0)
 
         regroup(1)
         nc.vector.quantize_mx(

@@ -187,8 +187,8 @@ def tile_vclinear_s_kernel(tc, inputs, W_wts, b_wts, out):
         for half in halves:
             accumulate(5, half)
         multiply(SDIM - 1, second)
-        for s in (6, 7):
-            for half in halves:
-                accumulate(s, half)
-
-        nc.sync.dma_start(out=out, in_=acc[:])
+        for half in halves:
+            accumulate(SDIM - 2, half)
+        for half in halves:
+            accumulate(SDIM - 1, half)
+            nc.sync.dma_start(out=out[:, half], in_=acc[:, half])

from contextlib import ExitStack

import concourse.mybir as mybir
from concourse.masks import make_identity

F32 = mybir.dt.float32
BF16 = mybir.dt.bfloat16
U32 = mybir.dt.uint32
U8 = mybir.dt.uint8
FP8X4 = mybir.dt.float8_e4m3fn_x4
ALU = mybir.AluOpType

P = 128
PACK = 4
B, I, O = 128, 512, 256
DEGREE = 3
KNOTS = (0.2, 0.4, 0.6, 0.8)
SDIM = DEGREE + 1 + len(KNOTS)
RUN = 4

VECTOR_OUTPUTS = (128, 96, 96, 80, 80, 72, 64, 24)

BIAS_PARTS = 4

FLOPS = 2 * SDIM * B * I * O + 2 * B * SDIM * O

assert I == P * PACK and B == P
assert all(abs(knot - (k + 1) * KNOTS[0]) < 1e-12 for k, knot in enumerate(KNOTS))


def regrouped(grouped, raw, outputs):
    dst = grouped[:, outputs, :].rearrange("p (c r) t -> p c t r", r=RUN)
    src = raw[:, :, outputs].rearrange("p t (c r) -> p c t r", r=RUN)
    return dst, src


def tile_vclinear_s_kernel(tc, inputs, W_wts, b_wts, out):
    nc = tc.nc
    with ExitStack() as ctx:
        ctx.enter_context(tc.manual_schedule())
        keep = ctx.enter_context(tc.tile_pool(name="keep", bufs=1))
        setup_psum = ctx.enter_context(tc.psum_pool(name="setup_psum", bufs=1))
        prod_psum = ctx.enter_context(tc.psum_pool(name="prod_psum", bufs=4))

        warm = keep.tile([P, 2], F32)
        nc.gpsimd.memset(warm[:, 0:1], 0.0)
        nc.scalar.copy(out=warm[:, 1:2], in_=warm[:, 0:1])

        t_sb = keep.tile([P, 32], BF16)
        nc.sync.dma_start(out=t_sb[:], in_=inputs[:, 0:32])
        t_col = t_sb[:, 0:1]
        b_bf = keep.tile([SDIM, O], BF16)
        nc.sync.dma_start(out=b_bf[:], in_=b_wts)
        x_sb = keep.tile([P, I], BF16)
        nc.sync.dma_start(out=x_sb[:], in_=inputs[:, 1 : 1 + I])
        w_dram = W_wts.rearrange("s (p t o) -> p s t o", p=P, t=PACK)
        w_raw = keep.tile([P, SDIM, PACK, O], BF16)
        for s in range(SDIM):
            nc.sync.dma_start(out=w_raw[:, s, :, :], in_=w_dram[:, s, :, :])

        ident = keep.tile([P, P], F32)
        make_identity(nc, ident[:])
        basis = keep.tile([P, P], F32)
        nc.vector.memset(basis[:], 0.0)
        nc.vector.memset(basis[:, 0:1], 1.0)
        b_f32 = keep.tile([P, O], F32)
        nc.vector.memset(b_f32[:], 0.0)
        knot_numbers = keep.tile([P, len(KNOTS)], F32)
        for k in range(len(KNOTS)):
            nc.vector.memset(knot_numbers[:, k : k + 1], float(k + 1))
        nc.scalar.copy(out=b_f32[0:SDIM, :], in_=b_bf[:])

        w_grouped = keep.tile([P, SDIM, O, PACK], BF16, align_bytes=64)
        w_codes = keep.tile([P, SDIM, O], U32, align_bytes=64)
        w_scales = keep.tile([P, SDIM, O], U8, align_bytes=64)
        x_codes = keep.tile([P, B], U32, align_bytes=64)
        x_scales = keep.tile([P, B], U8, align_bytes=64)
        acc = keep.tile([B, O], F32)
        prod_tiles = {}

        def regroup(s):
            split = VECTOR_OUTPUTS[s]
            dst, src = regrouped(w_grouped[:, s, :, :], w_raw[:, s, :, :], slice(0, split))
            nc.vector.tensor_copy(out=dst, in_=src)
            cuts = (split, O // 2, O) if s == SDIM - 1 else (split, O)
            for low, high in zip(cuts[:-1], cuts[1:]):
                dst, src = regrouped(w_grouped[:, s, :, :], w_raw[:, s, :, :], slice(low, high))
                nc.scalar.copy(out=dst, in_=src)

        def multiply(s, outputs=slice(0, O)):
            nc.vector.quantize_mx(
                out=w_codes[:, s, outputs].bitcast(FP8X4),
                scales=w_scales[:, s, outputs],
                in_=w_grouped[:, s, outputs, :].rearrange("p o t -> p (o t)"),
            )
            prod = prod_psum.tile([B, O], F32, name="prod")
            nc.tensor.matmul_mx(
                out=prod[:, outputs],
                lhsT=x_codes[:].bitcast(FP8X4),
                lhsT_scale=x_scales[:],
                rhs=w_codes[:, s, outputs].bitcast(FP8X4),
                rhs_scale=w_scales[:, s, outputs],
                start=True,
                stop=True,
            )
            for start in range(outputs.start, outputs.stop, O // 2):
                prod_tiles[(s, start)] = prod
            if 1 <= s < BIAS_PARTS:
                bias_matmul(s)

        def accumulate(s, outputs=slice(0, O)):
            if s == 0:
                nc.vector.tensor_scalar_mul(out=acc[:], in0=prod_tiles[(s, 0)][:], scalar1=basis[:, 0:1])
            else:
                nc.vector.scalar_tensor_tensor(
                    out=acc[:, outputs], in0=prod_tiles[(s, outputs.start)][:, outputs],
                    scalar=basis[:, s : s + 1],
                    in1=acc[:, outputs], op0=ALU.mult, op1=ALU.add,
                )

        distances = keep.tile([P, len(KNOTS)], F32)
        squares = keep.tile([P, len(KNOTS)], F32)
        nc.vector.scalar_tensor_tensor(
            out=distances[:], in0=knot_numbers[:], scalar=-KNOTS[0],
            in1=t_col.to_broadcast([P, len(KNOTS)]), op0=ALU.mult, op1=ALU.add,
        )
        nc.vector.tensor_copy(out=basis[:, 1:2], in_=t_col)
        nc.vector.scalar_tensor_tensor(
            out=squares[:], in0=distances[:], scalar=0.0, in1=distances[:], op0=ALU.max, op1=ALU.mult
        )
        nc.vector.tensor_scalar_mul(out=basis[:, 2:3], in0=t_col, scalar1=t_col)
        nc.vector.scalar_tensor_tensor(
            out=basis[:, DEGREE + 1 : SDIM], in0=distances[:], scalar=0.0, in1=squares[:],
            op0=ALU.max, op1=ALU.mult,
        )
        nc.vector.tensor_scalar(
            out=basis[:, 3:4], in0=t_col, scalar1=t_col, scalar2=t_col, op0=ALU.mult, op1=ALU.mult
        )

        x_words = x_sb[:].bitcast(F32).rearrange("p (w u) -> p u w", u=2)
        x_t = setup_psum.tile([P, 2, B], F32)
        for u in range(2):
            nc.tensor.transpose(x_t[:, u, :], x_words[:, u, :], ident[:])
        basis_t_psum = setup_psum.tile([P, B], F32)
        nc.tensor.transpose(basis_t_psum[:], basis[:], ident[:])
        x_grouped = keep.tile([P, B, PACK], BF16, align_bytes=64)
        regroup(0)
        nc.vector.tensor_copy(
            out=x_grouped[:].rearrange("p b t -> p (b t)").bitcast(F32).rearrange("p (b u) -> p b u", u=2),
            in_=x_t[:].rearrange("p u b -> p b u"),
        )

        basis_t = keep.tile([P, B], F32)
        nc.vector.tensor_copy(out=basis_t[:], in_=basis_t_psum[:])
        bias_psum = setup_psum.tile([B, O], F32)

        def bias_matmul(i):
            part = slice(i * (O // BIAS_PARTS), (i + 1) * (O // BIAS_PARTS))
            nc.tensor.matmul(
                bias_psum[:, part], lhsT=basis_t[:], rhs=b_f32[:, part], start=True, stop=True
            )

        bias_matmul(0)

        regroup(1)
        nc.vector.quantize_mx(
            out=x_codes[:].bitcast(FP8X4),
            scales=x_scales[:],
            in_=x_grouped[:].rearrange("p b t -> p (b t)"),
        )
        multiply(0)

        first, second = slice(0, O // 2), slice(O // 2, O)
        halves = (first, second)
        for step in range(2, SDIM - 1):
            regroup(step)
            if step >= 3:
                accumulate(step - 3)
            multiply(step - 1)
        regroup(SDIM - 1)
        for half in halves:
            nc.vector.tensor_add(out=acc[:, half], in0=acc[:, half], in1=bias_psum[:, half])
        multiply(SDIM - 2)
        for half in halves:
            accumulate(4, half)
        multiply(SDIM - 1, first)
        for half in halves:
            accumulate(5, half)
        multiply(SDIM - 1, second)
        for half in halves:
            accumulate(SDIM - 2, half)
        for half in halves:
            accumulate(SDIM - 1, half)
            nc.sync.dma_start(out=out[:, half], in_=acc[:, half])
